import numpy as np
import ml_dtypes


def mxq(x, axis, fmt="e4m3"):
    dtype, down = {"e4m3": (ml_dtypes.float8_e4m3fn, 7), "e5m2": (ml_dtypes.float8_e5m2, 14)}[fmt]
    v = np.moveaxis(np.asarray(x, np.float32).astype(ml_dtypes.bfloat16).astype(np.float64), axis, -1)
    blocks = v.reshape(v.shape[:-1] + (-1, 32))
    amax = np.abs(blocks).max(-1, keepdims=True)
    byte = np.maximum(np.where(amax > 0, np.frexp(amax)[1] - 1 + 127, 0) - down, 1)
    scale = np.exp2(byte - 127.0)
    codes = (blocks / scale).astype(np.float32).astype(dtype).astype(np.float64)
    return np.moveaxis((codes * scale).reshape(v.shape), -1, axis)


WIDE = False


def mx_kscale(k):
    if not WIDE:
        return np.ones(k)
    levels = np.array([10, -10, 5, -5, 0])
    if k % 512:
        return np.exp2(np.random.permutation(np.resize(levels, k // 32))).repeat(32)
    a = np.empty((k // 512, 16))
    for p in range(k // 512):
        a[p, :8] = np.random.permutation(np.resize(levels, 8))
        for g in range(8):
            far = levels[np.abs(levels - a[p, g]) >= 10]
            a[p, g + 8] = far[np.random.randint(len(far))]
    return np.exp2(a.ravel()).repeat(32)


BF16 = ml_dtypes.bfloat16


def bf(x):
    return np.asarray(x, np.float32).astype(BF16)


def f64(x):
    return np.asarray(x).astype(np.float64)


B, N, F, H, O = 16, 512, 512, 128, 512
BN_EPS = 1e-3


def setup_inputs():
    s, t = mx_kscale(F), mx_kscale(N)
    return {'x': bf(np.random.standard_normal((B, N, F)) * s / t[:, None]),
            'adj': bf(np.random.uniform(size=(B, N, N)) * (2.0 / N) * t),
            'w': bf(np.random.standard_normal((F, H)) * (0.22 * np.sqrt(N) / np.sqrt(F)) / s[:, None]),
            'bias': bf(np.random.standard_normal(H) * 0.1),
            'gamma': bf(1.0 + 0.1 * np.random.standard_normal(H)),
            'beta': bf(np.random.standard_normal(H) * 0.1),
            'mean': bf(np.random.standard_normal(H) * 0.1),
            'var': bf(0.01 + 0.02 * np.random.uniform(size=H))}


def reference(x, adj, w, bias, gamma, beta, mean, var):
    xw = mxq(f64(x), 2, 'e4m3') @ mxq(f64(w), 0, 'e4m3')
    agg = mxq(f64(adj), 2, 'e4m3') @ mxq(xw, 1, 'e4m3')
    h = np.maximum(agg + f64(bias), 0.0)
    return (h - f64(mean)) * (f64(gamma) / np.sqrt(f64(var) + BN_EPS)) + f64(beta)

@@ -1,0 +1,208 @@
+from contextlib import ExitStack
+
+import concourse.mybir as mybir
+from concourse.masks import make_identity
+
+F32 = mybir.dt.float32
+BF16 = mybir.dt.bfloat16
+U32 = mybir.dt.uint32
+U8 = mybir.dt.uint8
+FP8X4 = mybir.dt.float8_e4m3fn_x4
+ALU = mybir.AluOpType
+
+P = 128
+PACK = 4
+GRAPHS, NODES, FEATURES, HIDDEN = 16, 512, 512, 128
+BN_EPS = 1e-3
+FLOPS = 2 * GRAPHS * NODES * FEATURES * HIDDEN + 2 * GRAPHS * NODES * NODES * HIDDEN
+
+BIAS, GAMMA, BETA, MEAN, VAR = 0, 1, 2, 3, 4
+
+
+def tile_gnn_pa_t_kernel(tc, x, adj, w, bias, gamma, beta, mean, var, out):
+    nc = tc.nc
+    with ExitStack() as stack:
+        stack.enter_context(tc.manual_schedule())
+        const = stack.enter_context(tc.tile_pool(name="const", bufs=1))
+        resident = stack.enter_context(tc.tile_pool(name="resident", bufs=1))
+        work = stack.enter_context(tc.tile_pool(name="work", bufs=2))
+        psum_in = stack.enter_context(tc.psum_pool(name="psum_in", bufs=4))
+        psum_one = stack.enter_context(tc.psum_pool(name="psum_one", bufs=1))
+
+        x_sb = [resident.tile([P, PACK * FEATURES], BF16, name="x%d" % g) for g in range(GRAPHS)]
+        adj_sb = [resident.tile([P, PACK * NODES], BF16, name="adj%d" % g) for g in range(GRAPHS)]
+        for g in range(GRAPHS):
+            nc.sync.dma_start(out=x_sb[g][:], in_=x[g].rearrange("(p t) f -> p (t f)", t=PACK))
+            nc.sync.dma_start(out=adj_sb[g][:], in_=adj[g].rearrange("(p j) m -> p (j m)", j=PACK))
+
+        w_raw = const.tile([P, PACK, HIDDEN], BF16)
+        nc.scalar.dma_start(out=w_raw[:], in_=w.rearrange("(q t) h -> q t h", t=PACK))
+        vec_rows = const.tile([P, P], BF16)
+        nc.vector.memset(vec_rows[:], 0.0)
+        for row, vec in ((BIAS, bias), (GAMMA, gamma), (BETA, beta), (MEAN, mean), (VAR, var)):
+            nc.scalar.dma_start(out=vec_rows[row : row + 1, :], in_=vec.rearrange("(o h) -> o h", o=1))
+
+        ident = const.tile([P, P], F32)
+        make_identity(nc, ident[:])
+
+        warm_in = const.tile([P, 1], F32)
+        warm_out = const.tile([P, 1], F32)
+        nc.vector.memset(warm_in[:], 1.0)
+        nc.scalar.sqrt(out=warm_out[:], in_=warm_in[:])
+
+        w_grouped = const.tile([P, HIDDEN, PACK], BF16, align_bytes=64)
+        w_codes = const.tile([P, HIDDEN], U32, align_bytes=64)
+        w_scales = const.tile([P, HIDDEN], U8, align_bytes=64)
+        nc.vector.tensor_copy(out=w_grouped[:], in_=w_raw[:].rearrange("q t h -> q h t"))
+        vec_rows_f32 = const.tile([P, P], F32)
+        nc.vector.tensor_copy(out=vec_rows_f32[:], in_=vec_rows[:])
+        nc.vector.quantize_mx(
+            out=w_codes[:].bitcast(FP8X4), scales=w_scales[:], in_=w_grouped[:].rearrange("q h t -> q (h t)")
+        )
+
+        neg_bias = const.tile([P, 1], F32)
+        gain = const.tile([P, 1], F32)
+        shift_rep = const.tile([P, P], F32)
+        shift_rows = const.tile([P, P], F32)
+
+        def vectors_to_partitions():
+            vec_ps = psum_one.tile([P, P], F32, tag="setup")
+            nc.tensor.transpose(vec_ps[:], vec_rows_f32[:], ident[:])
+            vec_cols = const.tile([P, 8], F32)
+            nc.vector.tensor_copy(out=vec_cols[:], in_=vec_ps[:, 0:8])
+            var_eps = const.tile([P, 1], F32)
+            nc.vector.tensor_scalar_add(out=var_eps[:], in0=vec_cols[:, VAR : VAR + 1], scalar1=BN_EPS)
+            std = const.tile([P, 1], F32)
+            nc.scalar.sqrt(out=std[:], in_=var_eps[:])
+            nc.vector.tensor_scalar_mul(out=neg_bias[:], in0=vec_cols[:, BIAS : BIAS + 1], scalar1=-1.0)
+            centred = const.tile([P, 1], F32)
+            nc.vector.tensor_sub(out=centred[:], in0=vec_cols[:, BIAS : BIAS + 1], in1=vec_cols[:, MEAN : MEAN + 1])
+            inv_std = const.tile([P, 1], F32)
+            nc.vector.reciprocal(out=inv_std[:], in_=std[:])
+            nc.vector.tensor_mul(out=gain[:], in0=vec_cols[:, GAMMA : GAMMA + 1], in1=inv_std[:])
+            shift = const.tile([P, 1], F32)
+            nc.vector.tensor_scalar(
+                out=shift[:], in0=centred[:], scalar1=gain[:, 0:1], scalar2=vec_cols[:, BETA : BETA + 1],
+                op0=ALU.mult, op1=ALU.add,
+            )
+            nc.vector.tensor_copy(out=shift_rep[:], in_=shift[:, 0:1].to_broadcast([P, P]))
+
+        def shift_to_rows():
+            shift_ps = psum_one.tile([P, P], F32, tag="setup")
+            nc.tensor.transpose(shift_ps[:], shift_rep[:], ident[:])
+            nc.vector.tensor_copy(out=shift_rows[:], in_=shift_ps[:])
+
+        grouped = {}
+        quantised = {}
+        scaled = {}
+        result_ps = {}
+
+        def transpose_operand(name, g, rows_sb):
+            words = rows_sb[:].bitcast(F32)
+            tile_g = work.tile([P, PACK * 512], BF16, tag="%s_grouped" % name, name="%s_grouped" % name, align_bytes=64)
+            grouped_words = tile_g[:].bitcast(F32)
+            for pair in range(2):
+                bank = psum_in.tile([P, 2, 2 * P], F32, tag="bank", name="bank")
+                for half in range(2):
+                    for s in range(2):
+                        first = 256 * (2 * pair + s)
+                        nc.tensor.transpose(
+                            bank[:, half, P * s : P * (s + 1)], words[:, first + half : first + 256 : 2], ident[:]
+                        )
+                nc.scalar.copy(
+                    out=grouped_words[:, 512 * pair : 512 * (pair + 1)].rearrange("q (c half) -> q c half", half=2),
+                    in_=bank[:].rearrange("q half c -> q c half"),
+                )
+            grouped[(name, g)] = tile_g
+
+        def quantise(name, g, columns):
+            codes = work.tile([P, columns], U32, tag="%s_codes" % name, name="%s_codes" % name, align_bytes=64)
+            scales = work.tile([P, columns], U8, tag="%s_scales" % name, name="%s_scales" % name, align_bytes=64)
+            nc.vector.quantize_mx(out=codes[:].bitcast(FP8X4), scales=scales[:], in_=grouped[(name, g)][:])
+            quantised[(name, g)] = (codes, scales)
+
+        def first_product(g):
+            x_codes, x_scales = quantised[("x", g)]
+            xw_ps = psum_one.tile([P, PACK, HIDDEN], F32, tag="xw_ps")
+            for t in range(PACK):
+                nc.tensor.matmul_mx(
+                    out=xw_ps[:, t, :],
+                    lhsT=x_codes[:, P * t : P * (t + 1)].bitcast(FP8X4),
+                    lhsT_scale=x_scales[:, P * t : P * (t + 1)],
+                    rhs=w_codes[:].bitcast(FP8X4),
+                    rhs_scale=w_scales[:],
+                    start=True,
+                    stop=True,
+                )
+            xw_grouped = work.tile([P, HIDDEN * PACK], BF16, tag="xw_grouped", align_bytes=64)
+            nc.scalar.copy(
+                out=xw_grouped[:].rearrange("p (h t) -> p h t", t=PACK), in_=xw_ps[:].rearrange("p t h -> p h t")
+            )
+            grouped[("xw", g)] = xw_grouped
+
+        def second_product(g):
+            xw_codes, xw_scales = quantised[("xw", g)]
+            adj_codes, adj_scales = quantised[("adj", g)]
+            agg_ps = psum_one.tile([P, NODES], F32, tag="agg_ps")
+            nc.tensor.matmul_mx(
+                out=agg_ps[:],
+                lhsT=xw_codes[:].bitcast(FP8X4),
+                lhsT_scale=xw_scales[:],
+                rhs=adj_codes[:].bitcast(FP8X4),
+                rhs_scale=adj_scales[:],
+                start=True,
+                stop=True,
+            )
+            return agg_ps
+
+        def relu_and_gain(g, agg_ps):
+            scaled_sb = work.tile([P, NODES], F32, tag="scaled")
+            nc.vector.tensor_scalar(
+                out=scaled_sb[:], in0=agg_ps[:], scalar1=neg_bias[:, 0:1], scalar2=gain[:, 0:1],
+                op0=ALU.max, op1=ALU.mult,
+            )
+            scaled[g] = scaled_sb
+
+        def transpose_result(g):
+            res_ps = psum_one.tile([P, PACK, HIDDEN], F32, tag="res_ps")
+            for j in range(PACK):
+                nc.tensor.transpose(res_ps[:, j, :], scaled[g][:, P * j : P * (j + 1)], ident[:])
+            result_ps[g] = res_ps
+
+        def shift_and_store(g):
+            res_sb = resident.tile([P, PACK, HIDDEN], F32, name="res%d" % g)
+            nc.vector.tensor_tensor(
+                out=res_sb[:], in0=result_ps[g][:], in1=shift_rows[:].unsqueeze(1).to_broadcast([P, PACK, HIDDEN]),
+                op=ALU.add,
+            )
+            nc.sync.dma_start(
+                out=out[g].rearrange("(p j) h -> p (j h)", j=PACK), in_=res_sb[:].rearrange("p j h -> p (j h)")
+            )
+
+        def is_graph(g):
+            return 0 <= g < GRAPHS
+
+        for r in range(GRAPHS + 3):
+            if is_graph(r):
+                transpose_operand("x", r, x_sb[r])
+                transpose_operand("adj", r, adj_sb[r])
+            if is_graph(r - 3):
+                transpose_result(r - 3)
+            if r == 2:
+                shift_to_rows()
+            if is_graph(r - 1):
+                quantise("adj", r - 1, NODES)
+            if is_graph(r - 2):
+                quantise("xw", r - 2, HIDDEN)
+            if is_graph(r - 1):
+                first_product(r - 1)
+            if is_graph(r - 2):
+                agg_ps = second_product(r - 2)
+            if is_graph(r):
+                quantise("x", r, NODES)
+            if is_graph(r - 3):
+                shift_and_store(r - 3)
+            if is_graph(r - 2):
+                relu_and_gain(r - 2, agg_ps)
+            if r == 0:
+                vectors_to_partitions()

@@ -29,33 +29,35 @@ def tile_gnn_pa_t_kernel(tc, x, adj, w, bias, gamma, beta, mean, var, out):
         psum_in = stack.enter_context(tc.psum_pool(name="psum_in", bufs=4))
         psum_one = stack.enter_context(tc.psum_pool(name="psum_one", bufs=1))
 
-        x_sb = [resident.tile([P, PACK * FEATURES], BF16, name="x%d" % g) for g in range(GRAPHS)]
-        adj_sb = [resident.tile([P, PACK * NODES], BF16, name="adj%d" % g) for g in range(GRAPHS)]
-        for g in range(GRAPHS):
-            nc.sync.dma_start(out=x_sb[g][:], in_=x[g].rearrange("(p t) f -> p (t f)", t=PACK))
-            nc.sync.dma_start(out=adj_sb[g][:], in_=adj[g].rearrange("(p j) m -> p (j m)", j=PACK))
-
-        w_raw = const.tile([P, PACK, HIDDEN], BF16)
-        nc.scalar.dma_start(out=w_raw[:], in_=w.rearrange("(q t) h -> q t h", t=PACK))
-        vec_rows = const.tile([P, P], BF16)
-        nc.vector.memset(vec_rows[:], 0.0)
-        for row, vec in ((BIAS, bias), (GAMMA, gamma), (BETA, beta), (MEAN, mean), (VAR, var)):
-            nc.scalar.dma_start(out=vec_rows[row : row + 1, :], in_=vec.rearrange("(o h) -> o h", o=1))
-
-        ident = const.tile([P, P], F32)
-        make_identity(nc, ident[:])
-
         warm_in = const.tile([P, 1], F32)
         warm_out = const.tile([P, 1], F32)
         nc.vector.memset(warm_in[:], 1.0)
         nc.scalar.sqrt(out=warm_out[:], in_=warm_in[:])
 
+        vec_rows = const.tile([P, P], BF16)
+        nc.vector.memset(vec_rows[:], 0.0)
+        ident = const.tile([P, P], F32)
+        make_identity(nc, ident[:])
+        w_raw = const.tile([P, PACK, HIDDEN], BF16)
+        nc.gpsimd.dma_start(out=w_raw[:], in_=w.rearrange("(q t) h -> q t h", t=PACK))
+        for row, vec in ((BIAS, bias), (GAMMA, gamma), (BETA, beta), (MEAN, mean), (VAR, var)):
+            nc.gpsimd.dma_start(out=vec_rows[row : row + 1, :], in_=vec.rearrange("(o h) -> o h", o=1))
+
+        x_sb = [resident.tile([P, PACK * FEATURES], BF16, name="x%d" % g) for g in range(GRAPHS)]
+        adj_sb = [resident.tile([P, PACK * NODES], BF16, name="adj%d" % g) for g in range(GRAPHS)]
+        for t in range(PACK):
+            nc.sync.dma_start(
+                out=x_sb[0][:, FEATURES * t : FEATURES * (t + 1)], in_=x[0].rearrange("(p t) f -> p t f", t=PACK)[:, t, :]
+            )
+        for g in range(GRAPHS):
+            if g + 1 < GRAPHS:
+                nc.sync.dma_start(out=x_sb[g + 1][:], in_=x[g + 1].rearrange("(p t) f -> p (t f)", t=PACK))
+            nc.sync.dma_start(out=adj_sb[g][:], in_=adj[g].rearrange("(p j) m -> p (j m)", j=PACK))
+
         w_grouped = const.tile([P, HIDDEN, PACK], BF16, align_bytes=64)
         w_codes = const.tile([P, HIDDEN], U32, align_bytes=64)
         w_scales = const.tile([P, HIDDEN], U8, align_bytes=64)
         nc.vector.tensor_copy(out=w_grouped[:], in_=w_raw[:].rearrange("q t h -> q h t"))
-        vec_rows_f32 = const.tile([P, P], F32)
-        nc.vector.tensor_copy(out=vec_rows_f32[:], in_=vec_rows[:])
         nc.vector.quantize_mx(
             out=w_codes[:].bitcast(FP8X4), scales=w_scales[:], in_=w_grouped[:].rearrange("q h t -> q (h t)")
         )
@@ -66,6 +68,8 @@ def tile_gnn_pa_t_kernel(tc, x, adj, w, bias, gamma, beta, mean, var, out):
         shift_rows = const.tile([P, P], F32)
 
         def vectors_to_partitions():
+            vec_rows_f32 = const.tile([P, P], F32)
+            nc.vector.tensor_copy(out=vec_rows_f32[:], in_=vec_rows[:])
             vec_ps = psum_one.tile([P, P], F32, tag="setup")
             nc.tensor.transpose(vec_ps[:], vec_rows_f32[:], ident[:])
             vec_cols = const.tile([P, 8], F32)
@@ -95,6 +99,7 @@ def tile_gnn_pa_t_kernel(tc, x, adj, w, bias, gamma, beta, mean, var, out):
         grouped = {}
         quantised = {}
         scaled = {}
+        agg_banks = {}
         result_ps = {}
 
         def transpose_operand(name, g, rows_sb):
@@ -183,26 +188,26 @@ def tile_gnn_pa_t_kernel(tc, x, adj, w, bias, gamma, beta, mean, var, out):
             return 0 <= g < GRAPHS
 
         for r in range(GRAPHS + 3):
+            if is_graph(r - 3):
+                relu_and_gain(r - 3, agg_banks[r - 3])
+            if is_graph(r - 2):
+                quantise("xw", r - 2, HIDDEN)
+                quantise("adj", r - 2, NODES)
             if is_graph(r):
                 transpose_operand("x", r, x_sb[r])
-                transpose_operand("adj", r, adj_sb[r])
+            if is_graph(r - 1):
+                transpose_operand("adj", r - 1, adj_sb[r - 1])
             if is_graph(r - 3):
                 transpose_result(r - 3)
+            if is_graph(r):
+                quantise("x", r, NODES)
             if r == 2:
                 shift_to_rows()
             if is_graph(r - 1):
-                quantise("adj", r - 1, NODES)
-            if is_graph(r - 2):
-                quantise("xw", r - 2, HIDDEN)
-            if is_graph(r - 1):
                 first_product(r - 1)
             if is_graph(r - 2):
-                agg_ps = second_product(r - 2)
-            if is_graph(r):
-                quantise("x", r, NODES)
+                agg_banks[r - 2] = second_product(r - 2)
             if is_graph(r - 3):
                 shift_and_store(r - 3)
-            if is_graph(r - 2):
-                relu_and_gain(r - 2, agg_ps)
-            if r == 0:
+            if r == 1:
                 vectors_to_partitions()

@@ -38,10 +38,6 @@ def tile_gnn_pa_t_kernel(tc, x, adj, w, bias, gamma, beta, mean, var, out):
         nc.vector.memset(vec_rows[:], 0.0)
         ident = const.tile([P, P], F32)
         make_identity(nc, ident[:])
-        w_raw = const.tile([P, PACK, HIDDEN], BF16)
-        nc.gpsimd.dma_start(out=w_raw[:], in_=w.rearrange("(q t) h -> q t h", t=PACK))
-        for row, vec in ((BIAS, bias), (GAMMA, gamma), (BETA, beta), (MEAN, mean), (VAR, var)):
-            nc.gpsimd.dma_start(out=vec_rows[row : row + 1, :], in_=vec.rearrange("(o h) -> o h", o=1))
 
         x_sb = [resident.tile([P, PACK * FEATURES], BF16, name="x%d" % g) for g in range(GRAPHS)]
         adj_sb = [resident.tile([P, PACK * NODES], BF16, name="adj%d" % g) for g in range(GRAPHS)]
@@ -49,7 +45,12 @@ def tile_gnn_pa_t_kernel(tc, x, adj, w, bias, gamma, beta, mean, var, out):
             nc.sync.dma_start(
                 out=x_sb[0][:, FEATURES * t : FEATURES * (t + 1)], in_=x[0].rearrange("(p t) f -> p t f", t=PACK)[:, t, :]
             )
+        w_raw = const.tile([P, PACK, HIDDEN], BF16)
+        nc.scalar.dma_start(out=w_raw[:], in_=w.rearrange("(q t) h -> q t h", t=PACK))
         for g in range(GRAPHS):
+            if g == 1:
+                for row, vec in ((BIAS, bias), (GAMMA, gamma), (BETA, beta), (MEAN, mean), (VAR, var)):
+                    nc.sync.dma_start(out=vec_rows[row : row + 1, :], in_=vec.rearrange("(o h) -> o h", o=1))
             if g + 1 < GRAPHS:
                 nc.sync.dma_start(out=x_sb[g + 1][:], in_=x[g + 1].rearrange("(p t) f -> p (t f)", t=PACK))
             nc.sync.dma_start(out=adj_sb[g][:], in_=adj[g].rearrange("(p j) m -> p (j m)", j=PACK))

@@ -9,11 +9,13 @@ U32 = mybir.dt.uint32
 U8 = mybir.dt.uint8
 FP8X4 = mybir.dt.float8_e4m3fn_x4
 ALU = mybir.AluOpType
+ACT = mybir.ActivationFunctionType
 
 P = 128
 PACK = 4
 GRAPHS, NODES, FEATURES, HIDDEN = 16, 512, 512, 128
 BN_EPS = 1e-3
+SORTED = 2
 FLOPS = 2 * GRAPHS * NODES * FEATURES * HIDDEN + 2 * GRAPHS * NODES * NODES * HIDDEN
 
 BIAS, GAMMA, BETA, MEAN, VAR = 0, 1, 2, 3, 4
@@ -63,7 +65,9 @@ def tile_gnn_pa_t_kernel(tc, x, adj, w, bias, gamma, beta, mean, var, out):
             out=w_codes[:].bitcast(FP8X4), scales=w_scales[:], in_=w_grouped[:].rearrange("q h t -> q (h t)")
         )
 
+        bias_col = const.tile([P, 1], F32)
         neg_bias = const.tile([P, 1], F32)
+        neg_gain_bias = const.tile([P, 1], F32)
         gain = const.tile([P, 1], F32)
         shift_rep = const.tile([P, P], F32)
         shift_rows = const.tile([P, P], F32)
@@ -71,7 +75,7 @@ def tile_gnn_pa_t_kernel(tc, x, adj, w, bias, gamma, beta, mean, var, out):
         def vectors_to_partitions():
             vec_rows_f32 = const.tile([P, P], F32)
             nc.vector.tensor_copy(out=vec_rows_f32[:], in_=vec_rows[:])
-            vec_ps = psum_one.tile([P, P], F32, tag="setup")
+            vec_ps = psum_one.tile([P, P], F32, tag="spare")
             nc.tensor.transpose(vec_ps[:], vec_rows_f32[:], ident[:])
             vec_cols = const.tile([P, 8], F32)
             nc.vector.tensor_copy(out=vec_cols[:], in_=vec_ps[:, 0:8])
@@ -85,6 +89,8 @@ def tile_gnn_pa_t_kernel(tc, x, adj, w, bias, gamma, beta, mean, var, out):
             inv_std = const.tile([P, 1], F32)
             nc.vector.reciprocal(out=inv_std[:], in_=std[:])
             nc.vector.tensor_mul(out=gain[:], in0=vec_cols[:, GAMMA : GAMMA + 1], in1=inv_std[:])
+            nc.vector.tensor_copy(out=bias_col[:], in_=vec_cols[:, BIAS : BIAS + 1])
+            nc.vector.tensor_mul(out=neg_gain_bias[:], in0=gain[:], in1=neg_bias[:])
             shift = const.tile([P, 1], F32)
             nc.vector.tensor_scalar(
                 out=shift[:], in0=centred[:], scalar1=gain[:, 0:1], scalar2=vec_cols[:, BETA : BETA + 1],
@@ -93,17 +99,26 @@ def tile_gnn_pa_t_kernel(tc, x, adj, w, bias, gamma, beta, mean, var, out):
             nc.vector.tensor_copy(out=shift_rep[:], in_=shift[:, 0:1].to_broadcast([P, P]))
 
         def shift_to_rows():
-            shift_ps = psum_one.tile([P, P], F32, tag="setup")
+            shift_ps = psum_one.tile([P, P], F32, tag="spare")
             nc.tensor.transpose(shift_ps[:], shift_rep[:], ident[:])
             nc.vector.tensor_copy(out=shift_rows[:], in_=shift_ps[:])
 
         grouped = {}
+        x_sorted = {}
         quantised = {}
         scaled = {}
         agg_banks = {}
         result_ps = {}
 
-        def transpose_operand(name, g, rows_sb):
+        def sort_words(g):
+            tile_g = work.tile([P, SORTED * FEATURES], BF16, tag="x_sorted")
+            nc.vector.tensor_copy(
+                out=tile_g[:].bitcast(F32).rearrange("p (s e m) -> p s e m", e=2, m=P),
+                in_=x_sb[g][:, 0 : SORTED * FEATURES].bitcast(F32).rearrange("p (s m e) -> p s e m", e=2, m=P),
+            )
+            x_sorted[g] = tile_g[:].bitcast(F32)
+
+        def transpose_operand(name, g, rows_sb, sorted_words=None):
             words = rows_sb[:].bitcast(F32)
             tile_g = work.tile([P, PACK * 512], BF16, tag="%s_grouped" % name, name="%s_grouped" % name, align_bytes=64)
             grouped_words = tile_g[:].bitcast(F32)
@@ -112,24 +127,31 @@ def tile_gnn_pa_t_kernel(tc, x, adj, w, bias, gamma, beta, mean, var, out):
                 for half in range(2):
                     for s in range(2):
                         first = 256 * (2 * pair + s)
-                        nc.tensor.transpose(
-                            bank[:, half, P * s : P * (s + 1)], words[:, first + half : first + 256 : 2], ident[:]
-                        )
+                        if sorted_words is not None and 2 * pair + s < SORTED:
+                            part = sorted_words[:, first + P * half : first + P * (half + 1)]
+                        else:
+                            part = words[:, first + half : first + 256 : 2]
+                        nc.tensor.transpose(bank[:, half, P * s : P * (s + 1)], part, ident[:])
                 nc.scalar.copy(
                     out=grouped_words[:, 512 * pair : 512 * (pair + 1)].rearrange("q (c half) -> q c half", half=2),
                     in_=bank[:].rearrange("q half c -> q c half"),
                 )
             grouped[(name, g)] = tile_g
 
-        def quantise(name, g, columns):
-            codes = work.tile([P, columns], U32, tag="%s_codes" % name, name="%s_codes" % name, align_bytes=64)
-            scales = work.tile([P, columns], U8, tag="%s_scales" % name, name="%s_scales" % name, align_bytes=64)
-            nc.vector.quantize_mx(out=codes[:].bitcast(FP8X4), scales=scales[:], in_=grouped[(name, g)][:])
-            quantised[(name, g)] = (codes, scales)
+        def quantise(name, g, columns, first=0, part=""):
+            tag = name + part
+            codes = work.tile([P, columns], U32, tag="%s_codes" % tag, name="%s_codes" % tag, align_bytes=64)
+            scales = work.tile([P, columns], U8, tag="%s_scales" % tag, name="%s_scales" % tag, align_bytes=64)
+            nc.vector.quantize_mx(
+                out=codes[:].bitcast(FP8X4),
+                scales=scales[:],
+                in_=grouped[(name, g)][:, PACK * first : PACK * (first + columns)],
+            )
+            quantised[(name + part, g)] = (codes, scales)
 
         def first_product(g):
             x_codes, x_scales = quantised[("x", g)]
-            xw_ps = psum_one.tile([P, PACK, HIDDEN], F32, tag="xw_ps")
+            xw_ps = psum_one.tile([P, PACK, HIDDEN], F32, tag="spare" if g == GRAPHS - 1 else "xw_ps")
             for t in range(PACK):
                 nc.tensor.matmul_mx(
                     out=xw_ps[:, t, :],
@@ -146,10 +168,10 @@ def tile_gnn_pa_t_kernel(tc, x, adj, w, bias, gamma, beta, mean, var, out):
             )
             grouped[("xw", g)] = xw_grouped
 
-        def second_product(g):
+        def second_product(g, part="", bank="agg_ps"):
             xw_codes, xw_scales = quantised[("xw", g)]
-            adj_codes, adj_scales = quantised[("adj", g)]
-            agg_ps = psum_one.tile([P, NODES], F32, tag="agg_ps")
+            adj_codes, adj_scales = quantised[("adj" + part, g)]
+            agg_ps = psum_one.tile([P, adj_codes.shape[1]], F32, tag=bank, name="agg_ps")
             nc.tensor.matmul_mx(
                 out=agg_ps[:],
                 lhsT=xw_codes[:].bitcast(FP8X4),
@@ -161,47 +183,60 @@ def tile_gnn_pa_t_kernel(tc, x, adj, w, bias, gamma, beta, mean, var, out):
             )
             return agg_ps
 
-        def relu_and_gain(g, agg_ps):
-            scaled_sb = work.tile([P, NODES], F32, tag="scaled")
+        def relu_and_gain(agg_ps):
+            scaled_sb = work.tile([P, agg_ps.shape[1]], F32, tag="scaled", bufs=3)
             nc.vector.tensor_scalar(
                 out=scaled_sb[:], in0=agg_ps[:], scalar1=neg_bias[:, 0:1], scalar2=gain[:, 0:1],
                 op0=ALU.max, op1=ALU.mult,
             )
-            scaled[g] = scaled_sb
+            return scaled_sb
 
-        def transpose_result(g):
-            res_ps = psum_one.tile([P, PACK, HIDDEN], F32, tag="res_ps")
-            for j in range(PACK):
-                nc.tensor.transpose(res_ps[:, j, :], scaled[g][:, P * j : P * (j + 1)], ident[:])
-            result_ps[g] = res_ps
+        def relu_and_gain_scalar(agg_ps):
+            relu_sb = work.tile([P, NODES], F32, tag="relu")
+            nc.scalar.activation(out=relu_sb[:], in_=agg_ps[:], func=ACT.Relu, bias=bias_col[:, 0:1])
+            scaled_sb = work.tile([P, NODES], F32, tag="scaled", bufs=3)
+            nc.scalar.activation(
+                out=scaled_sb[:], in_=relu_sb[:], func=ACT.Identity, scale=gain[:, 0:1], bias=neg_gain_bias[:, 0:1]
+            )
+            return scaled_sb
 
-        def shift_and_store(g):
-            res_sb = resident.tile([P, PACK, HIDDEN], F32, name="res%d" % g)
+        def transpose_result(scaled_sb, res_ps):
+            for j in range(res_ps.shape[1]):
+                nc.tensor.transpose(res_ps[:, j, :], scaled_sb[:, P * j : P * (j + 1)], ident[:])
+            return res_ps
+
+        def shift_and_store(g, res_ps, first=0):
+            slots = res_ps.shape[1]
+            res_sb = resident.tile([P, slots, HIDDEN], F32, name="res%d_%d" % (g, first))
             nc.vector.tensor_tensor(
-                out=res_sb[:], in0=result_ps[g][:], in1=shift_rows[:].unsqueeze(1).to_broadcast([P, PACK, HIDDEN]),
+                out=res_sb[:], in0=res_ps[:], in1=shift_rows[:].unsqueeze(1).to_broadcast([P, slots, HIDDEN]),
                 op=ALU.add,
             )
             nc.sync.dma_start(
-                out=out[g].rearrange("(p j) h -> p (j h)", j=PACK), in_=res_sb[:].rearrange("p j h -> p (j h)")
+                out=out[g].rearrange("(p j) h -> p j h", j=PACK)[:, first : first + slots, :], in_=res_sb[:]
             )
+
+        def result_bank():
+            return psum_one.tile([P, PACK, HIDDEN], F32, tag="res_ps", name="res_ps")
 
         def is_graph(g):
             return 0 <= g < GRAPHS
 
-        for r in range(GRAPHS + 3):
+        last = GRAPHS - 1
+        for r in range(GRAPHS):
             if is_graph(r - 3):
-                relu_and_gain(r - 3, agg_banks[r - 3])
+                scaled[r - 3] = relu_and_gain(agg_banks[r - 3])
+            if r > 0 and is_graph(r + 1):
+                sort_words(r + 1)
             if is_graph(r - 2):
                 quantise("xw", r - 2, HIDDEN)
                 quantise("adj", r - 2, NODES)
-            if is_graph(r):
-                transpose_operand("x", r, x_sb[r])
+            transpose_operand("x", r, x_sb[r], x_sorted.get(r))
             if is_graph(r - 1):
                 transpose_operand("adj", r - 1, adj_sb[r - 1])
             if is_graph(r - 3):
-                transpose_result(r - 3)
-            if is_graph(r):
-                quantise("x", r, NODES)
+                result_ps[r - 3] = transpose_result(scaled[r - 3], result_bank())
+            quantise("x", r, NODES)
             if r == 2:
                 shift_to_rows()
             if is_graph(r - 1):
@@ -209,6 +244,30 @@ def tile_gnn_pa_t_kernel(tc, x, adj, w, bias, gamma, beta, mean, var, out):
             if is_graph(r - 2):
                 agg_banks[r - 2] = second_product(r - 2)
             if is_graph(r - 3):
-                shift_and_store(r - 3)
+                shift_and_store(r - 3, result_ps[r - 3])
             if r == 1:
                 vectors_to_partitions()
+
+        first_product(last)
+        scaled[last - 2] = relu_and_gain(agg_banks[last - 2])
+        quantise("xw", last - 1, HIDDEN)
+        quantise("adj", last - 1, NODES)
+        transpose_operand("adj", last, adj_sb[last])
+        result_ps[last - 2] = transpose_result(scaled[last - 2], result_bank())
+        quantise("xw", last, HIDDEN)
+        agg_banks[last - 1] = second_product(last - 1)
+        half = NODES // 2
+        quantise("adj", last, half, 0, "_lo")
+        agg_lo = second_product(last, "_lo", "xw_ps")
+        shift_and_store(last - 2, result_ps[last - 2])
+        scaled[last - 1] = relu_and_gain_scalar(agg_banks[last - 1])
+        quantise("adj", last, half, half, "_hi")
+        result_ps[last - 1] = transpose_result(scaled[last - 1], result_bank())
+        agg_hi = second_product(last, "_hi", "spare")
+        scaled_lo = relu_and_gain(agg_lo)
+        scaled_hi = relu_and_gain(agg_hi)
+        res_lo = transpose_result(scaled_lo, psum_in.tile([P, 2, HIDDEN], F32, tag="bank", name="res_lo"))
+        res_hi = transpose_result(scaled_hi, psum_in.tile([P, 2, HIDDEN], F32, tag="bank", name="res_hi"))
+        shift_and_store(last - 1, result_ps[last - 1])
+        shift_and_store(last, res_lo, 0)
+        shift_and_store(last, res_hi, 2)

@@ -15,7 +15,7 @@ P = 128
 PACK = 4
 GRAPHS, NODES, FEATURES, HIDDEN = 16, 512, 512, 128
 BN_EPS = 1e-3
-SORTED = 2
+SORTED = 1
 FLOPS = 2 * GRAPHS * NODES * FEATURES * HIDDEN + 2 * GRAPHS * NODES * NODES * HIDDEN
 
 BIAS, GAMMA, BETA, MEAN, VAR = 0, 1, 2, 3, 4
@@ -226,11 +226,11 @@ def tile_gnn_pa_t_kernel(tc, x, adj, w, bias, gamma, beta, mean, var, out):
         for r in range(GRAPHS):
             if is_graph(r - 3):
                 scaled[r - 3] = relu_and_gain(agg_banks[r - 3])
-            if r > 0 and is_graph(r + 1):
-                sort_words(r + 1)
             if is_graph(r - 2):
                 quantise("xw", r - 2, HIDDEN)
                 quantise("adj", r - 2, NODES)
+            if r > 0 and is_graph(r + 1):
+                sort_words(r + 1)
             transpose_operand("x", r, x_sb[r], x_sorted.get(r))
             if is_graph(r - 1):
                 transpose_operand("adj", r - 1, adj_sb[r - 1])
@@ -262,8 +262,8 @@ def tile_gnn_pa_t_kernel(tc, x, adj, w, bias, gamma, beta, mean, var, out):
         shift_and_store(last - 2, result_ps[last - 2])
         scaled[last - 1] = relu_and_gain_scalar(agg_banks[last - 1])
         quantise("adj", last, half, half, "_hi")
-        result_ps[last - 1] = transpose_result(scaled[last - 1], result_bank())
         agg_hi = second_product(last, "_hi", "spare")
+        result_ps[last - 1] = transpose_result(scaled[last - 1], result_bank())
         scaled_lo = relu_and_gain(agg_lo)
         scaled_hi = relu_and_gain(agg_hi)
         res_lo = transpose_result(scaled_lo, psum_in.tile([P, 2, HIDDEN], F32, tag="bank", name="res_lo"))

@@ -52,7 +52,7 @@ def tile_gnn_pa_t_kernel(tc, x, adj, w, bias, gamma, beta, mean, var, out):
         for g in range(GRAPHS):
             if g == 1:
                 for row, vec in ((BIAS, bias), (GAMMA, gamma), (BETA, beta), (MEAN, mean), (VAR, var)):
-                    nc.sync.dma_start(out=vec_rows[row : row + 1, :], in_=vec.rearrange("(o h) -> o h", o=1))
+                    nc.scalar.dma_start(out=vec_rows[row : row + 1, :], in_=vec.rearrange("(o h) -> o h", o=1))
             if g + 1 < GRAPHS:
                 nc.sync.dma_start(out=x_sb[g + 1][:], in_=x[g + 1].rearrange("(p t) f -> p (t f)", t=PACK))
             nc.sync.dma_start(out=adj_sb[g][:], in_=adj[g].rearrange("(p j) m -> p (j m)", j=PACK))
@@ -67,41 +67,41 @@ def tile_gnn_pa_t_kernel(tc, x, adj, w, bias, gamma, beta, mean, var, out):
 
         bias_col = const.tile([P, 1], F32)
         neg_bias = const.tile([P, 1], F32)
-        neg_gain_bias = const.tile([P, 1], F32)
+        offset = const.tile([P, 1], F32)
         gain = const.tile([P, 1], F32)
         shift_rep = const.tile([P, P], F32)
         shift_rows = const.tile([P, P], F32)
 
+        vec_rows_f32 = const.tile([P, P], F32)
+        vec_cols = const.tile([P, 8], F32)
+        std = const.tile([P, 1], F32)
+        centred = const.tile([P, 1], F32)
+
         def vectors_to_partitions():
-            vec_rows_f32 = const.tile([P, P], F32)
-            nc.vector.tensor_copy(out=vec_rows_f32[:], in_=vec_rows[:])
             vec_ps = psum_one.tile([P, P], F32, tag="spare")
             nc.tensor.transpose(vec_ps[:], vec_rows_f32[:], ident[:])
-            vec_cols = const.tile([P, 8], F32)
             nc.vector.tensor_copy(out=vec_cols[:], in_=vec_ps[:, 0:8])
             var_eps = const.tile([P, 1], F32)
             nc.vector.tensor_scalar_add(out=var_eps[:], in0=vec_cols[:, VAR : VAR + 1], scalar1=BN_EPS)
-            std = const.tile([P, 1], F32)
             nc.scalar.sqrt(out=std[:], in_=var_eps[:])
             nc.vector.tensor_scalar_mul(out=neg_bias[:], in0=vec_cols[:, BIAS : BIAS + 1], scalar1=-1.0)
-            centred = const.tile([P, 1], F32)
             nc.vector.tensor_sub(out=centred[:], in0=vec_cols[:, BIAS : BIAS + 1], in1=vec_cols[:, MEAN : MEAN + 1])
+
+        def gain_and_shift():
             inv_std = const.tile([P, 1], F32)
             nc.vector.reciprocal(out=inv_std[:], in_=std[:])
             nc.vector.tensor_mul(out=gain[:], in0=vec_cols[:, GAMMA : GAMMA + 1], in1=inv_std[:])
-            nc.vector.tensor_copy(out=bias_col[:], in_=vec_cols[:, BIAS : BIAS + 1])
-            nc.vector.tensor_mul(out=neg_gain_bias[:], in0=gain[:], in1=neg_bias[:])
             shift = const.tile([P, 1], F32)
             nc.vector.tensor_scalar(
                 out=shift[:], in0=centred[:], scalar1=gain[:, 0:1], scalar2=vec_cols[:, BETA : BETA + 1],
                 op0=ALU.mult, op1=ALU.add,
             )
             nc.vector.tensor_copy(out=shift_rep[:], in_=shift[:, 0:1].to_broadcast([P, P]))
+            nc.vector.tensor_copy(out=bias_col[:], in_=vec_cols[:, BIAS : BIAS + 1])
+            mean_gain = const.tile([P, 1], F32)
+            nc.vector.tensor_mul(out=mean_gain[:], in0=vec_cols[:, MEAN : MEAN + 1], in1=gain[:])
+            nc.vector.tensor_sub(out=offset[:], in0=vec_cols[:, BETA : BETA + 1], in1=mean_gain[:])
 
-        def shift_to_rows():
-            shift_ps = psum_one.tile([P, P], F32, tag="spare")
-            nc.tensor.transpose(shift_ps[:], shift_rep[:], ident[:])
-            nc.vector.tensor_copy(out=shift_rows[:], in_=shift_ps[:])
 
         grouped = {}
         x_sorted = {}
@@ -191,12 +191,12 @@ def tile_gnn_pa_t_kernel(tc, x, adj, w, bias, gamma, beta, mean, var, out):
             )
             return scaled_sb
 
-        def relu_and_gain_scalar(agg_ps):
+        def finish_on_scalar(agg_ps):
             relu_sb = work.tile([P, NODES], F32, tag="relu")
             nc.scalar.activation(out=relu_sb[:], in_=agg_ps[:], func=ACT.Relu, bias=bias_col[:, 0:1])
             scaled_sb = work.tile([P, NODES], F32, tag="scaled", bufs=3)
             nc.scalar.activation(
-                out=scaled_sb[:], in_=relu_sb[:], func=ACT.Identity, scale=gain[:, 0:1], bias=neg_gain_bias[:, 0:1]
+                out=scaled_sb[:], in_=relu_sb[:], func=ACT.Identity, scale=gain[:, 0:1], bias=offset[:, 0:1]
             )
             return scaled_sb
 
@@ -208,10 +208,13 @@ def tile_gnn_pa_t_kernel(tc, x, adj, w, bias, gamma, beta, mean, var, out):
         def shift_and_store(g, res_ps, first=0):
             slots = res_ps.shape[1]
             res_sb = resident.tile([P, slots, HIDDEN], F32, name="res%d_%d" % (g, first))
-            nc.vector.tensor_tensor(
-                out=res_sb[:], in0=res_ps[:], in1=shift_rows[:].unsqueeze(1).to_broadcast([P, slots, HIDDEN]),
-                op=ALU.add,
-            )
+            if g == GRAPHS - 2:
+                nc.scalar.copy(out=res_sb[:], in_=res_ps[:])
+            else:
+                nc.vector.tensor_tensor(
+                    out=res_sb[:], in0=res_ps[:], in1=shift_rows[:].unsqueeze(1).to_broadcast([P, slots, HIDDEN]),
+                    op=ALU.add,
+                )
             nc.sync.dma_start(
                 out=out[g].rearrange("(p j) h -> p j h", j=PACK)[:, first : first + slots, :], in_=res_sb[:]
             )
@@ -231,20 +234,27 @@ def tile_gnn_pa_t_kernel(tc, x, adj, w, bias, gamma, beta, mean, var, out):
                 quantise("adj", r - 2, NODES)
             if r > 0 and is_graph(r + 1):
                 sort_words(r + 1)
+            if r == 2:
+                gain_and_shift()
             transpose_operand("x", r, x_sb[r], x_sorted.get(r))
             if is_graph(r - 1):
                 transpose_operand("adj", r - 1, adj_sb[r - 1])
+            if r == 3:
+                shift_ps = psum_one.tile([P, P], F32, tag="spare", name="shift_ps")
+                nc.tensor.transpose(shift_ps[:], shift_rep[:], ident[:])
             if is_graph(r - 3):
                 result_ps[r - 3] = transpose_result(scaled[r - 3], result_bank())
             quantise("x", r, NODES)
-            if r == 2:
-                shift_to_rows()
+            if r == 3:
+                nc.vector.tensor_copy(out=shift_rows[:], in_=shift_ps[:])
             if is_graph(r - 1):
                 first_product(r - 1)
             if is_graph(r - 2):
                 agg_banks[r - 2] = second_product(r - 2)
             if is_graph(r - 3):
                 shift_and_store(r - 3, result_ps[r - 3])
+            if r == 0:
+                nc.vector.tensor_copy(out=vec_rows_f32[:], in_=vec_rows[:])
             if r == 1:
                 vectors_to_partitions()
 
@@ -260,14 +270,14 @@ def tile_gnn_pa_t_kernel(tc, x, adj, w, bias, gamma, beta, mean, var, out):
         quantise("adj", last, half, 0, "_lo")
         agg_lo = second_product(last, "_lo", "xw_ps")
         shift_and_store(last - 2, result_ps[last - 2])
-        scaled[last - 1] = relu_and_gain_scalar(agg_banks[last - 1])
+        scaled[last - 1] = finish_on_scalar(agg_banks[last - 1])
         quantise("adj", last, half, half, "_hi")
         agg_hi = second_product(last, "_hi", "spare")
-        result_ps[last - 1] = transpose_result(scaled[last - 1], result_bank())
         scaled_lo = relu_and_gain(agg_lo)
         scaled_hi = relu_and_gain(agg_hi)
         res_lo = transpose_result(scaled_lo, psum_in.tile([P, 2, HIDDEN], F32, tag="bank", name="res_lo"))
         res_hi = transpose_result(scaled_hi, psum_in.tile([P, 2, HIDDEN], F32, tag="bank", name="res_hi"))
-        shift_and_store(last - 1, result_ps[last - 1])
+        result_ps[last - 1] = transpose_result(scaled[last - 1], result_bank())
         shift_and_store(last, res_lo, 0)
         shift_and_store(last, res_hi, 2)
+        shift_and_store(last - 1, result_ps[last - 1])

@@ -43,17 +43,18 @@ def tile_gnn_pa_t_kernel(tc, x, adj, w, bias, gamma, beta, mean, var, out):
 
         x_sb = [resident.tile([P, PACK * FEATURES], BF16, name="x%d" % g) for g in range(GRAPHS)]
         adj_sb = [resident.tile([P, PACK * NODES], BF16, name="adj%d" % g) for g in range(GRAPHS)]
-        for t in range(PACK):
+        for g, first, slots in ((0, 0, 1), (0, 1, 1), (0, 2, 2), (1, 0, 2), (1, 2, 2)):
             nc.sync.dma_start(
-                out=x_sb[0][:, FEATURES * t : FEATURES * (t + 1)], in_=x[0].rearrange("(p t) f -> p t f", t=PACK)[:, t, :]
+                out=x_sb[g][:].rearrange("p (t f) -> p t f", t=PACK)[:, first : first + slots, :],
+                in_=x[g].rearrange("(p t) f -> p t f", t=PACK)[:, first : first + slots, :],
             )
         w_raw = const.tile([P, PACK, HIDDEN], BF16)
         nc.scalar.dma_start(out=w_raw[:], in_=w.rearrange("(q t) h -> q t h", t=PACK))
         for g in range(GRAPHS):
             if g == 1:
                 for row, vec in ((BIAS, bias), (GAMMA, gamma), (BETA, beta), (MEAN, mean), (VAR, var)):
-                    nc.scalar.dma_start(out=vec_rows[row : row + 1, :], in_=vec.rearrange("(o h) -> o h", o=1))
-            if g + 1 < GRAPHS:
+                    nc.sync.dma_start(out=vec_rows[row : row + 1, :], in_=vec.rearrange("(o h) -> o h", o=1))
+            if 0 < g < GRAPHS - 1:
                 nc.sync.dma_start(out=x_sb[g + 1][:], in_=x[g + 1].rearrange("(p t) f -> p (t f)", t=PACK))
             nc.sync.dma_start(out=adj_sb[g][:], in_=adj[g].rearrange("(p j) m -> p (j m)", j=PACK))
 
@@ -87,24 +88,31 @@ def tile_gnn_pa_t_kernel(tc, x, adj, w, bias, gamma, beta, mean, var, out):
             nc.vector.tensor_scalar_mul(out=neg_bias[:], in0=vec_cols[:, BIAS : BIAS + 1], scalar1=-1.0)
             nc.vector.tensor_sub(out=centred[:], in0=vec_cols[:, BIAS : BIAS + 1], in1=vec_cols[:, MEAN : MEAN + 1])
 
-        def gain_and_shift():
-            inv_std = const.tile([P, 1], F32)
+        inv_std = const.tile([P, 1], F32)
+        shift = const.tile([P, 1], F32)
+        mean_gain = const.tile([P, 1], F32)
+
+        def invert_root():
             nc.vector.reciprocal(out=inv_std[:], in_=std[:])
+
+        def make_gain():
             nc.vector.tensor_mul(out=gain[:], in0=vec_cols[:, GAMMA : GAMMA + 1], in1=inv_std[:])
-            shift = const.tile([P, 1], F32)
+
+        def make_shift():
             nc.vector.tensor_scalar(
                 out=shift[:], in0=centred[:], scalar1=gain[:, 0:1], scalar2=vec_cols[:, BETA : BETA + 1],
                 op0=ALU.mult, op1=ALU.add,
             )
+            nc.vector.tensor_mul(out=mean_gain[:], in0=vec_cols[:, MEAN : MEAN + 1], in1=gain[:])
+
+        def widen_shift():
             nc.vector.tensor_copy(out=shift_rep[:], in_=shift[:, 0:1].to_broadcast([P, P]))
             nc.vector.tensor_copy(out=bias_col[:], in_=vec_cols[:, BIAS : BIAS + 1])
-            mean_gain = const.tile([P, 1], F32)
-            nc.vector.tensor_mul(out=mean_gain[:], in0=vec_cols[:, MEAN : MEAN + 1], in1=gain[:])
             nc.vector.tensor_sub(out=offset[:], in0=vec_cols[:, BETA : BETA + 1], in1=mean_gain[:])
-
 
         grouped = {}
         x_sorted = {}
+        postponed = []
         quantised = {}
         scaled = {}
         agg_banks = {}
@@ -118,7 +126,7 @@ def tile_gnn_pa_t_kernel(tc, x, adj, w, bias, gamma, beta, mean, var, out):
             )
             x_sorted[g] = tile_g[:].bitcast(F32)
 
-        def transpose_operand(name, g, rows_sb, sorted_words=None):
+        def transpose_operand(name, g, rows_sb, sorted_words=None, copies=(nc.scalar.copy, nc.scalar.copy)):
             words = rows_sb[:].bitcast(F32)
             tile_g = work.tile([P, PACK * 512], BF16, tag="%s_grouped" % name, name="%s_grouped" % name, align_bytes=64)
             grouped_words = tile_g[:].bitcast(F32)
@@ -132,11 +140,19 @@ def tile_gnn_pa_t_kernel(tc, x, adj, w, bias, gamma, beta, mean, var, out):
                         else:
                             part = words[:, first + half : first + 256 : 2]
                         nc.tensor.transpose(bank[:, half, P * s : P * (s + 1)], part, ident[:])
-                nc.scalar.copy(
+                copies[pair](
                     out=grouped_words[:, 512 * pair : 512 * (pair + 1)].rearrange("q (c half) -> q c half", half=2),
                     in_=bank[:].rearrange("q half c -> q c half"),
                 )
             grouped[(name, g)] = tile_g
+
+        def copy_later(out, in_):
+            postponed.append((out, in_))
+
+        def copy_postponed():
+            for out_ap, in_ap in postponed:
+                nc.vector.tensor_copy(out=out_ap, in_=in_ap)
+            postponed.clear()
 
         def quantise(name, g, columns, first=0, part=""):
             tag = name + part
@@ -168,10 +184,11 @@ def tile_gnn_pa_t_kernel(tc, x, adj, w, bias, gamma, beta, mean, var, out):
             )
             grouped[("xw", g)] = xw_grouped
 
-        def second_product(g, part="", bank="agg_ps"):
+        def second_product(g, part="", bank="agg_ps", agg_ps=None):
             xw_codes, xw_scales = quantised[("xw", g)]
             adj_codes, adj_scales = quantised[("adj" + part, g)]
-            agg_ps = psum_one.tile([P, adj_codes.shape[1]], F32, tag=bank, name="agg_ps")
+            if agg_ps is None:
+                agg_ps = psum_one.tile([P, adj_codes.shape[1]], F32, tag=bank, name="agg_ps")
             nc.tensor.matmul_mx(
                 out=agg_ps[:],
                 lhsT=xw_codes[:].bitcast(FP8X4),
@@ -230,21 +247,29 @@ def tile_gnn_pa_t_kernel(tc, x, adj, w, bias, gamma, beta, mean, var, out):
             if is_graph(r - 3):
                 scaled[r - 3] = relu_and_gain(agg_banks[r - 3])
             if is_graph(r - 2):
-                quantise("xw", r - 2, HIDDEN)
                 quantise("adj", r - 2, NODES)
-            if r > 0 and is_graph(r + 1):
+                if r == 2:
+                    invert_root()
+                quantise("xw", r - 2, HIDDEN)
+                if r == 2:
+                    make_gain()
+            if r > 1 and is_graph(r + 2):
                 sort_words(r + 1)
             if r == 2:
-                gain_and_shift()
+                make_shift()
             transpose_operand("x", r, x_sb[r], x_sorted.get(r))
             if is_graph(r - 1):
-                transpose_operand("adj", r - 1, adj_sb[r - 1])
+                second_copy = copy_later if r == 1 else nc.scalar.copy
+                transpose_operand("adj", r - 1, adj_sb[r - 1], copies=(nc.scalar.copy, second_copy))
             if r == 3:
                 shift_ps = psum_one.tile([P, P], F32, tag="spare", name="shift_ps")
                 nc.tensor.transpose(shift_ps[:], shift_rep[:], ident[:])
             if is_graph(r - 3):
                 result_ps[r - 3] = transpose_result(scaled[r - 3], result_bank())
             quantise("x", r, NODES)
+            copy_postponed()
+            if r == 2:
+                widen_shift()
             if r == 3:
                 nc.vector.tensor_copy(out=shift_rows[:], in_=shift_ps[:])
             if is_graph(r - 1):
@@ -259,25 +284,26 @@ def tile_gnn_pa_t_kernel(tc, x, adj, w, bias, gamma, beta, mean, var, out):
                 vectors_to_partitions()
 
         first_product(last)
-        scaled[last - 2] = relu_and_gain(agg_banks[last - 2])
-        quantise("xw", last - 1, HIDDEN)
         quantise("adj", last - 1, NODES)
+        quantise("xw", last - 1, HIDDEN)
+        scaled[last - 2] = relu_and_gain(agg_banks[last - 2])
         transpose_operand("adj", last, adj_sb[last])
+        agg_banks[last - 1] = second_product(last - 1, agg_ps=psum_in.tile([P, NODES], F32, tag="bank", name="agg_ps"))
         result_ps[last - 2] = transpose_result(scaled[last - 2], result_bank())
         quantise("xw", last, HIDDEN)
-        agg_banks[last - 1] = second_product(last - 1)
         half = NODES // 2
         quantise("adj", last, half, 0, "_lo")
         agg_lo = second_product(last, "_lo", "xw_ps")
-        shift_and_store(last - 2, result_ps[last - 2])
         scaled[last - 1] = finish_on_scalar(agg_banks[last - 1])
         quantise("adj", last, half, half, "_hi")
         agg_hi = second_product(last, "_hi", "spare")
         scaled_lo = relu_and_gain(agg_lo)
         scaled_hi = relu_and_gain(agg_hi)
+        shift_and_store(last - 2, result_ps[last - 2])
         res_lo = transpose_result(scaled_lo, psum_in.tile([P, 2, HIDDEN], F32, tag="bank", name="res_lo"))
         res_hi = transpose_result(scaled_hi, psum_in.tile([P, 2, HIDDEN], F32, tag="bank", name="res_hi"))
-        result_ps[last - 1] = transpose_result(scaled[last - 1], result_bank())
+        res_full = psum_in.tile([P, PACK, HIDDEN], F32, tag="bank", name="res_full")
+        result_ps[last - 1] = transpose_result(scaled[last - 1], res_full)
         shift_and_store(last, res_lo, 0)
         shift_and_store(last, res_hi, 2)
         shift_and_store(last - 1, result_ps[last - 1])

from contextlib import ExitStack

import concourse.mybir as mybir
from concourse.masks import make_identity

F32 = mybir.dt.float32
BF16 = mybir.dt.bfloat16
U32 = mybir.dt.uint32
U8 = mybir.dt.uint8
FP8X4 = mybir.dt.float8_e4m3fn_x4
ALU = mybir.AluOpType
ACT = mybir.ActivationFunctionType

P = 128
PACK = 4
GRAPHS, NODES, FEATURES, HIDDEN = 16, 512, 512, 128
BN_EPS = 1e-3
SORTED = 1
FLOPS = 2 * GRAPHS * NODES * FEATURES * HIDDEN + 2 * GRAPHS * NODES * NODES * HIDDEN

BIAS, GAMMA, BETA, MEAN, VAR = 0, 1, 2, 3, 4


def tile_gnn_pa_t_kernel(tc, x, adj, w, bias, gamma, beta, mean, var, out):
    nc = tc.nc
    with ExitStack() as stack:
        stack.enter_context(tc.manual_schedule())
        const = stack.enter_context(tc.tile_pool(name="const", bufs=1))
        resident = stack.enter_context(tc.tile_pool(name="resident", bufs=1))
        work = stack.enter_context(tc.tile_pool(name="work", bufs=2))
        psum_in = stack.enter_context(tc.psum_pool(name="psum_in", bufs=4))
        psum_one = stack.enter_context(tc.psum_pool(name="psum_one", bufs=1))

        warm_in = const.tile([P, 1], F32)
        warm_out = const.tile([P, 1], F32)
        nc.vector.memset(warm_in[:], 1.0)
        nc.scalar.sqrt(out=warm_out[:], in_=warm_in[:])

        vec_rows = const.tile([P, P], BF16)
        nc.vector.memset(vec_rows[:], 0.0)
        ident = const.tile([P, P], F32)
        make_identity(nc, ident[:])

        x_sb = [resident.tile([P, PACK * FEATURES], BF16, name="x%d" % g) for g in range(GRAPHS)]
        adj_sb = [resident.tile([P, PACK * NODES], BF16, name="adj%d" % g) for g in range(GRAPHS)]
        for g, first, slots in ((0, 0, 1), (0, 1, 1), (0, 2, 2), (1, 0, 2), (1, 2, 2)):
            nc.sync.dma_start(
                out=x_sb[g][:].rearrange("p (t f) -> p t f", t=PACK)[:, first : first + slots, :],
                in_=x[g].rearrange("(p t) f -> p t f", t=PACK)[:, first : first + slots, :],
            )
        w_raw = const.tile([P, PACK, HIDDEN], BF16)
        nc.scalar.dma_start(out=w_raw[:], in_=w.rearrange("(q t) h -> q t h", t=PACK))
        for g in range(GRAPHS):
            if g == 1:
                for row, vec in ((BIAS, bias), (GAMMA, gamma), (BETA, beta), (MEAN, mean), (VAR, var)):
                    nc.sync.dma_start(out=vec_rows[row : row + 1, :], in_=vec.rearrange("(o h) -> o h", o=1))
            if 0 < g < GRAPHS - 1:
                nc.sync.dma_start(out=x_sb[g + 1][:], in_=x[g + 1].rearrange("(p t) f -> p (t f)", t=PACK))
            nc.sync.dma_start(out=adj_sb[g][:], in_=adj[g].rearrange("(p j) m -> p (j m)", j=PACK))

        w_grouped = const.tile([P, HIDDEN, PACK], BF16, align_bytes=64)
        w_codes = const.tile([P, HIDDEN], U32, align_bytes=64)
        w_scales = const.tile([P, HIDDEN], U8, align_bytes=64)
        nc.vector.tensor_copy(out=w_grouped[:], in_=w_raw[:].rearrange("q t h -> q h t"))
        nc.vector.quantize_mx(
            out=w_codes[:].bitcast(FP8X4), scales=w_scales[:], in_=w_grouped[:].rearrange("q h t -> q (h t)")
        )

        bias_col = const.tile([P, 1], F32)
        neg_bias = const.tile([P, 1], F32)
        offset = const.tile([P, 1], F32)
        gain = const.tile([P, 1], F32)
        shift_rep = const.tile([P, P], F32)
        shift_rows = const.tile([P, P], F32)

        vec_rows_f32 = const.tile([P, P], F32)
        vec_cols = const.tile([P, 8], F32)
        std = const.tile([P, 1], F32)
        centred = const.tile([P, 1], F32)

        def vectors_to_partitions():
            vec_ps = psum_one.tile([P, P], F32, tag="spare")
            nc.tensor.transpose(vec_ps[:], vec_rows_f32[:], ident[:])
            nc.vector.tensor_copy(out=vec_cols[:], in_=vec_ps[:, 0:8])
            var_eps = const.tile([P, 1], F32)
            nc.vector.tensor_scalar_add(out=var_eps[:], in0=vec_cols[:, VAR : VAR + 1], scalar1=BN_EPS)
            nc.scalar.sqrt(out=std[:], in_=var_eps[:])
            nc.vector.tensor_scalar_mul(out=neg_bias[:], in0=vec_cols[:, BIAS : BIAS + 1], scalar1=-1.0)
            nc.vector.tensor_sub(out=centred[:], in0=vec_cols[:, BIAS : BIAS + 1], in1=vec_cols[:, MEAN : MEAN + 1])

        inv_std = const.tile([P, 1], F32)
        shift = const.tile([P, 1], F32)
        mean_gain = const.tile([P, 1], F32)

        def invert_root():
            nc.vector.reciprocal(out=inv_std[:], in_=std[:])

        def make_gain():
            nc.vector.tensor_mul(out=gain[:], in0=vec_cols[:, GAMMA : GAMMA + 1], in1=inv_std[:])

        def make_shift():
            nc.vector.tensor_scalar(
                out=shift[:], in0=centred[:], scalar1=gain[:, 0:1], scalar2=vec_cols[:, BETA : BETA + 1],
                op0=ALU.mult, op1=ALU.add,
            )
            nc.vector.tensor_mul(out=mean_gain[:], in0=vec_cols[:, MEAN : MEAN + 1], in1=gain[:])

        def widen_shift():
            nc.vector.tensor_copy(out=shift_rep[:], in_=shift[:, 0:1].to_broadcast([P, P]))
            nc.vector.tensor_copy(out=bias_col[:], in_=vec_cols[:, BIAS : BIAS + 1])
            nc.vector.tensor_sub(out=offset[:], in0=vec_cols[:, BETA : BETA + 1], in1=mean_gain[:])

        grouped = {}
        x_sorted = {}
        postponed = []
        quantised = {}
        scaled = {}
        agg_banks = {}
        result_ps = {}

        def sort_words(g):
            tile_g = work.tile([P, SORTED * FEATURES], BF16, tag="x_sorted")
            nc.vector.tensor_copy(
                out=tile_g[:].bitcast(F32).rearrange("p (s e m) -> p s e m", e=2, m=P),
                in_=x_sb[g][:, 0 : SORTED * FEATURES].bitcast(F32).rearrange("p (s m e) -> p s e m", e=2, m=P),
            )
            x_sorted[g] = tile_g[:].bitcast(F32)

        def transpose_operand(name, g, rows_sb, sorted_words=None, copies=(nc.scalar.copy, nc.scalar.copy)):
            words = rows_sb[:].bitcast(F32)
            tile_g = work.tile([P, PACK * 512], BF16, tag="%s_grouped" % name, name="%s_grouped" % name, align_bytes=64)
            grouped_words = tile_g[:].bitcast(F32)
            for pair in range(2):
                bank = psum_in.tile([P, 2, 2 * P], F32, tag="bank", name="bank")
                for half in range(2):
                    for s in range(2):
                        first = 256 * (2 * pair + s)
                        if sorted_words is not None and 2 * pair + s < SORTED:
                            part = sorted_words[:, first + P * half : first + P * (half + 1)]
                        else:
                            part = words[:, first + half : first + 256 : 2]
                        nc.tensor.transpose(bank[:, half, P * s : P * (s + 1)], part, ident[:])
                copies[pair](
                    out=grouped_words[:, 512 * pair : 512 * (pair + 1)].rearrange("q (c half) -> q c half", half=2),
                    in_=bank[:].rearrange("q half c -> q c half"),
                )
            grouped[(name, g)] = tile_g

        def copy_later(out, in_):
            postponed.append((out, in_))

        def copy_postponed():
            for out_ap, in_ap in postponed:
                nc.vector.tensor_copy(out=out_ap, in_=in_ap)
            postponed.clear()

        def quantise(name, g, columns, first=0, part=""):
            tag = name + part
            codes = work.tile([P, columns], U32, tag="%s_codes" % tag, name="%s_codes" % tag, align_bytes=64)
            scales = work.tile([P, columns], U8, tag="%s_scales" % tag, name="%s_scales" % tag, align_bytes=64)
            nc.vector.quantize_mx(
                out=codes[:].bitcast(FP8X4),
                scales=scales[:],
                in_=grouped[(name, g)][:, PACK * first : PACK * (first + columns)],
            )
            quantised[(name + part, g)] = (codes, scales)

        def first_product(g):
            x_codes, x_scales = quantised[("x", g)]
            xw_ps = psum_one.tile([P, PACK, HIDDEN], F32, tag="spare" if g == GRAPHS - 1 else "xw_ps")
            for t in range(PACK):
                nc.tensor.matmul_mx(
                    out=xw_ps[:, t, :],
                    lhsT=x_codes[:, P * t : P * (t + 1)].bitcast(FP8X4),
                    lhsT_scale=x_scales[:, P * t : P * (t + 1)],
                    rhs=w_codes[:].bitcast(FP8X4),
                    rhs_scale=w_scales[:],
                    start=True,
                    stop=True,
                )
            xw_grouped = work.tile([P, HIDDEN * PACK], BF16, tag="xw_grouped", align_bytes=64)
            nc.scalar.copy(
                out=xw_grouped[:].rearrange("p (h t) -> p h t", t=PACK), in_=xw_ps[:].rearrange("p t h -> p h t")
            )
            grouped[("xw", g)] = xw_grouped

        def second_product(g, part="", bank="agg_ps", agg_ps=None):
            xw_codes, xw_scales = quantised[("xw", g)]
            adj_codes, adj_scales = quantised[("adj" + part, g)]
            if agg_ps is None:
                agg_ps = psum_one.tile([P, adj_codes.shape[1]], F32, tag=bank, name="agg_ps")
            nc.tensor.matmul_mx(
                out=agg_ps[:],
                lhsT=xw_codes[:].bitcast(FP8X4),
                lhsT_scale=xw_scales[:],
                rhs=adj_codes[:].bitcast(FP8X4),
                rhs_scale=adj_scales[:],
                start=True,
                stop=True,
            )
            return agg_ps

        def relu_and_gain(agg_ps):
            scaled_sb = work.tile([P, agg_ps.shape[1]], F32, tag="scaled", bufs=3)
            nc.vector.tensor_scalar(
                out=scaled_sb[:], in0=agg_ps[:], scalar1=neg_bias[:, 0:1], scalar2=gain[:, 0:1],
                op0=ALU.max, op1=ALU.mult,
            )
            return scaled_sb

        def finish_on_scalar(agg_ps):
            relu_sb = work.tile([P, NODES], F32, tag="relu")
            nc.scalar.activation(out=relu_sb[:], in_=agg_ps[:], func=ACT.Relu, bias=bias_col[:, 0:1])
            scaled_sb = work.tile([P, NODES], F32, tag="scaled", bufs=3)
            nc.scalar.activation(
                out=scaled_sb[:], in_=relu_sb[:], func=ACT.Identity, scale=gain[:, 0:1], bias=offset[:, 0:1]
            )
            return scaled_sb

        def transpose_result(scaled_sb, res_ps):
            for j in range(res_ps.shape[1]):
                nc.tensor.transpose(res_ps[:, j, :], scaled_sb[:, P * j : P * (j + 1)], ident[:])
            return res_ps

        def shift_and_store(g, res_ps, first=0):
            slots = res_ps.shape[1]
            res_sb = resident.tile([P, slots, HIDDEN], F32, name="res%d_%d" % (g, first))
            if g == GRAPHS - 2:
                nc.scalar.copy(out=res_sb[:], in_=res_ps[:])
            else:
                nc.vector.tensor_tensor(
                    out=res_sb[:], in0=res_ps[:], in1=shift_rows[:].unsqueeze(1).to_broadcast([P, slots, HIDDEN]),
                    op=ALU.add,
                )
            nc.sync.dma_start(
                out=out[g].rearrange("(p j) h -> p j h", j=PACK)[:, first : first + slots, :], in_=res_sb[:]
            )

        def result_bank():
            return psum_one.tile([P, PACK, HIDDEN], F32, tag="res_ps", name="res_ps")

        def is_graph(g):
            return 0 <= g < GRAPHS

        last = GRAPHS - 1
        for r in range(GRAPHS):
            if is_graph(r - 3):
                scaled[r - 3] = relu_and_gain(agg_banks[r - 3])
            if is_graph(r - 2):
                quantise("adj", r - 2, NODES)
                if r == 2:
                    invert_root()
                quantise("xw", r - 2, HIDDEN)
                if r == 2:
                    make_gain()
            if r > 1 and is_graph(r + 2):
                sort_words(r + 1)
            if r == 2:
                make_shift()
            transpose_operand("x", r, x_sb[r], x_sorted.get(r))
            if is_graph(r - 1):
                second_copy = copy_later if r == 1 else nc.scalar.copy
                transpose_operand("adj", r - 1, adj_sb[r - 1], copies=(nc.scalar.copy, second_copy))
            if r == 3:
                shift_ps = psum_one.tile([P, P], F32, tag="spare", name="shift_ps")
                nc.tensor.transpose(shift_ps[:], shift_rep[:], ident[:])
            if is_graph(r - 3):
                result_ps[r - 3] = transpose_result(scaled[r - 3], result_bank())
            quantise("x", r, NODES)
            copy_postponed()
            if r == 2:
                widen_shift()
            if r == 3:
                nc.vector.tensor_copy(out=shift_rows[:], in_=shift_ps[:])
            if is_graph(r - 1):
                first_product(r - 1)
            if is_graph(r - 2):
                agg_banks[r - 2] = second_product(r - 2)
            if is_graph(r - 3):
                shift_and_store(r - 3, result_ps[r - 3])
            if r == 0:
                nc.vector.tensor_copy(out=vec_rows_f32[:], in_=vec_rows[:])
            if r == 1:
                vectors_to_partitions()

        first_product(last)
        quantise("adj", last - 1, NODES)
        quantise("xw", last - 1, HIDDEN)
        scaled[last - 2] = relu_and_gain(agg_banks[last - 2])
        transpose_operand("adj", last, adj_sb[last])
        agg_banks[last - 1] = second_product(last - 1, agg_ps=psum_in.tile([P, NODES], F32, tag="bank", name="agg_ps"))
        result_ps[last - 2] = transpose_result(scaled[last - 2], result_bank())
        quantise("xw", last, HIDDEN)
        half = NODES // 2
        quantise("adj", last, half, 0, "_lo")
        agg_lo = second_product(last, "_lo", "xw_ps")
        scaled[last - 1] = finish_on_scalar(agg_banks[last - 1])
        quantise("adj", last, half, half, "_hi")
        agg_hi = second_product(last, "_hi", "spare")
        scaled_lo = relu_and_gain(agg_lo)
        scaled_hi = relu_and_gain(agg_hi)
        shift_and_store(last - 2, result_ps[last - 2])
        res_lo = transpose_result(scaled_lo, psum_in.tile([P, 2, HIDDEN], F32, tag="bank", name="res_lo"))
        res_hi = transpose_result(scaled_hi, psum_in.tile([P, 2, HIDDEN], F32, tag="bank", name="res_hi"))
        res_full = psum_in.tile([P, PACK, HIDDEN], F32, tag="bank", name="res_full")
        result_ps[last - 1] = transpose_result(scaled[last - 1], res_full)
        shift_and_store(last, res_lo, 0)
        shift_and_store(last, res_hi, 2)
        shift_and_store(last - 1, result_ps[last - 1])
